import numpy as np
import ml_dtypes


def mxq(x, axis, fmt="e4m3"):
    dtype, down = {"e4m3": (ml_dtypes.float8_e4m3fn, 7), "e5m2": (ml_dtypes.float8_e5m2, 14)}[fmt]
    v = np.moveaxis(np.asarray(x, np.float32).astype(ml_dtypes.bfloat16).astype(np.float64), axis, -1)
    blocks = v.reshape(v.shape[:-1] + (-1, 32))
    amax = np.abs(blocks).max(-1, keepdims=True)
    byte = np.maximum(np.where(amax > 0, np.frexp(amax)[1] - 1 + 127, 0) - down, 1)
    scale = np.exp2(byte - 127.0)
    codes = (blocks / scale).astype(np.float32).astype(dtype).astype(np.float64)
    return np.moveaxis((codes * scale).reshape(v.shape), -1, axis)


WIDE = False


def mx_kscale(k):
    if not WIDE:
        return np.ones(k)
    levels = np.array([10, -10, 5, -5, 0])
    if k % 512:
        return np.exp2(np.random.permutation(np.resize(levels, k // 32))).repeat(32)
    a = np.empty((k // 512, 16))
    for p in range(k // 512):
        a[p, :8] = np.random.permutation(np.resize(levels, 8))
        for g in range(8):
            far = levels[np.abs(levels - a[p, g]) >= 10]
            a[p, g + 8] = far[np.random.randint(len(far))]
    return np.exp2(a.ravel()).repeat(32)


BF16 = ml_dtypes.bfloat16


def bf(x):
    return np.asarray(x, np.float32).astype(BF16)


def f64(x):
    return np.asarray(x).astype(np.float64)


B, N, DI, D, H, DO = 2, 512, 1024, 1024, 16, 1024
DH = D // H
SIG = 0.5


def time_concat(space):
    t = np.sqrt(1.0 + np.sum(space * space, axis=-1, keepdims=True))
    return np.concatenate([t, space], axis=-1)


def split_lift(space):
    return time_concat(space.reshape(B, N, H, DH).transpose(0, 2, 1, 3))


def setup_inputs():
    s = mx_kscale(DI)
    return {"x_space": bf(np.random.standard_normal((B, N, DI)) * s),
            "Wq": bf(np.random.standard_normal((D, DI)) * SIG / np.sqrt(DI) / s),
            "bq": bf(np.random.standard_normal(D) * 0.1),
            "Wk": bf(np.random.standard_normal((D, DI)) * SIG / np.sqrt(DI) / s),
            "bk": bf(np.random.standard_normal(D) * 0.1)}


def reference(x_space, Wq, bq, Wk, bk):
    xq = mxq(f64(x_space), 2, "e4m3")
    q = (xq @ mxq(f64(Wq), 1, "e4m3").T) + f64(bq)
    k = (xq @ mxq(f64(Wk), 1, "e4m3").T) + f64(bk)
    return split_lift(q), split_lift(k)

@@ -1,0 +1,245 @@
+from contextlib import ExitStack
+
+import concourse.mybir as mybir
+from concourse.masks import make_identity
+
+F32 = mybir.dt.float32
+BF16 = mybir.dt.bfloat16
+U32 = mybir.dt.uint32
+U8 = mybir.dt.uint8
+FP8X4 = mybir.dt.float8_e4m3fn_x4
+ACT = mybir.ActivationFunctionType
+ALU = mybir.AluOpType
+AXIS = mybir.AxisListType
+
+P = 128
+BATCH, TOKENS, K = 2, 512, 1024
+FEATURES, HEAD_DIM = 1024, 64
+LIFTED = HEAD_DIM + 1
+PACK = 4
+K_PASS = P * PACK
+PASSES = K // K_PASS
+HALVES = 2
+ROW_WORDS = K // 2
+BLOCKS = 2
+UNIT_ROWS = BLOCKS * P
+J = BATCH * TOKENS // P
+X_UNITS = J // BLOCKS
+CHUNK_HEADS = UNIT_ROWS // HEAD_DIM
+W_UNITS = FEATURES // UNIT_ROWS
+CHUNKS = 2 * W_UNITS
+POOL_UNIT = 0
+STEPS = CHUNKS * X_UNITS
+BANK = 512
+
+FLOPS = 2 * BATCH * TOKENS * K * 2 * FEATURES
+
+
+def tile_lorentzmultiheadattention_pa_kernel(tc, x_space, Wq, bq, Wk, bk, out_0, out_1):
+    nc = tc.nc
+    weights = (Wq, Wk)
+    biases = (bq, bk)
+    outputs = (out_0, out_1)
+
+    with ExitStack() as ctx:
+        consts = ctx.enter_context(tc.tile_pool(name="consts", bufs=1))
+        raw_pool = ctx.enter_context(tc.tile_pool(name="raw", bufs=1))
+        mx_pool = ctx.enter_context(tc.tile_pool(name="mx", bufs=1))
+        stage = ctx.enter_context(tc.tile_pool(name="stage", bufs=4))
+        out_pool = ctx.enter_context(tc.tile_pool(name="outp", bufs=CHUNKS))
+        scratch = ctx.enter_context(tc.tile_pool(name="scratch", bufs=4))
+        flip_psum = ctx.enter_context(tc.psum_pool(name="flip", bufs=4))
+        acc_psum = ctx.enter_context(tc.psum_pool(name="acc", bufs=4))
+        ctx.enter_context(tc.manual_schedule())
+
+        one = consts.tile([P, 1], F32)
+        nc.vector.memset(one[:], 1.0)
+        root = consts.tile([P, 1], F32)
+        nc.scalar.activation(out=root[:], in_=one[:], func=ACT.Sqrt)
+        ident = consts.tile([P, P], F32)
+        make_identity(nc, ident[:])
+        ones = consts.tile([P, P], BF16)
+        nc.vector.memset(ones[:], 1.0)
+        bias_rows = consts.tile([P, 2, FEATURES], BF16)
+        nc.vector.memset(bias_rows[:], 0.0)
+
+        def load_x(unit):
+            raw = raw_pool.tile([P, BLOCKS * K], BF16, name="raw_x%d" % unit)
+            for b in range(BATCH):
+                rows = x_space[b].rearrange("(p j) k -> p (j k)", j=J)
+                nc.sync.dma_start(
+                    out=raw[b:P:BATCH, :],
+                    in_=rows[:, unit * BLOCKS * K : (unit + 1) * BLOCKS * K],
+                )
+            return raw
+
+        def load_w(chunk):
+            raw = raw_pool.tile([P, BLOCKS * K], BF16, name="raw_w%d" % chunk)
+            rows = weights[chunk // W_UNITS].rearrange("(c b r) k -> c r b k", b=BLOCKS, r=P)
+            nc.sync.dma_start(
+                out=raw[:].rearrange("p (b k) -> p b k", b=BLOCKS),
+                in_=rows[chunk % W_UNITS],
+            )
+            return raw
+
+        order = [("x", 0), ("w", 0)]
+        order.extend([("x", unit) for unit in range(1, X_UNITS)])
+        order.extend([("w", chunk) for chunk in range(1, CHUNKS)])
+        raw = {}
+        for kind, n in order:
+            raw[(kind, n)] = load_x(n) if kind == "x" else load_w(n)
+            if (kind, n) == ("w", 0):
+                for w in range(2):
+                    nc.sync.dma_start(out=bias_rows[0:1, w, :], in_=biases[w].unsqueeze(0))
+
+        def flip(raw, vector_helps=True):
+            words = raw[:].bitcast(F32)
+            grouped = stage.tile([P, PASSES * UNIT_ROWS * PACK], BF16, align_bytes=64, tag="grouped")
+            grouped_words = grouped[:].bitcast(F32).rearrange(
+                "p (g b r u) -> p g b r u", g=PASSES, b=BLOCKS, u=HALVES
+            )
+            for b in range(BLOCKS):
+                flipped = flip_psum.tile([P, PASSES, HALVES, P], F32, tag="flip")
+                for g in range(PASSES):
+                    for u in range(HALVES):
+                        first = b * ROW_WORDS + g * HALVES * P + u
+                        nc.tensor.transpose(
+                            flipped[:, g, u, :], words[:, first : first + HALVES * P - 1 : HALVES], ident[:]
+                        )
+                source = flipped[:].rearrange("p g u r -> p g r u")
+                if b == 1 and vector_helps:
+                    nc.vector.tensor_copy(out=grouped_words[:, :, b, :, :], in_=source)
+                else:
+                    nc.scalar.copy(out=grouped_words[:, :, b, :, :], in_=source)
+            return grouped
+
+        def quantise(grouped, key):
+            name = "%s%d" % key
+            codes = mx_pool.tile([P, PASSES, UNIT_ROWS], U32, align_bytes=64, name="codes_" + name)
+            scales = mx_pool.tile([P, PASSES, UNIT_ROWS], U8, align_bytes=64, name="scales_" + name)
+            nc.vector.quantize_mx(
+                out=codes[:].rearrange("p g r -> p (g r)").bitcast(FP8X4),
+                scales=scales[:].rearrange("p g r -> p (g r)"),
+                in_=grouped[:],
+            )
+            return codes, scales
+
+        bias = consts.tile([P, 2, FEATURES], BF16)
+
+        def spread_bias(w):
+            spread = acc_psum.tile([P, FEATURES], BF16, tag="acc")
+            for q in range(FEATURES // BANK):
+                cols = slice(q * BANK, (q + 1) * BANK)
+                nc.tensor.matmul(
+                    out=spread[:, cols], lhsT=ones[:], rhs=bias_rows[:, w, cols], start=True, stop=True
+                )
+            nc.scalar.copy(out=bias[:, w, :], in_=spread[:])
+
+        mx = {}
+        lifted = [None] * CHUNKS
+        norms = [None] * CHUNKS
+        pool_squares = [None] * CHUNKS
+
+        def project(chunk, unit):
+            x_codes, x_scales = mx[("x", unit)]
+            w_codes, w_scales = mx[("w", chunk)]
+            acc = acc_psum.tile([P, BLOCKS, UNIT_ROWS], F32, tag="acc")
+            for b in range(BLOCKS):
+                tokens = slice(b * P, (b + 1) * P)
+                for g in range(PASSES):
+                    nc.tensor.matmul_mx(
+                        out=acc[:, b, :],
+                        lhsT=x_codes[:, g, tokens].bitcast(FP8X4),
+                        lhsT_scale=x_scales[:, g, tokens],
+                        rhs=w_codes[:, g, :].bitcast(FP8X4),
+                        rhs_scale=w_scales[:, g, :],
+                        start=(g == 0),
+                        stop=(g == PASSES - 1),
+                    )
+            return acc
+
+        def add_bias(chunk, unit, acc):
+            first = (chunk % W_UNITS) * UNIT_ROWS
+            bias_chunk = bias[:, chunk // W_UNITS, first : first + UNIT_ROWS].rearrange(
+                "p (h d) -> p h d", d=HEAD_DIM
+            )
+            j0 = unit * BLOCKS
+            nc.vector.tensor_tensor(
+                out=lifted[chunk][:, :, j0 : j0 + BLOCKS, 1:LIFTED],
+                in0=acc[:].rearrange("p b (h d) -> p h b d", d=HEAD_DIM),
+                in1=bias_chunk.unsqueeze(2).to_broadcast([P, CHUNK_HEADS, BLOCKS, HEAD_DIM]),
+                op=ALU.add,
+            )
+
+        def scalar_norms(chunk, heads, tokens):
+            squares = scratch.tile([P, len(heads), len(tokens), HEAD_DIM], F32, tag="squares")
+            for row, h in enumerate(heads):
+                for col, j in enumerate(tokens):
+                    nc.scalar.activation(
+                        out=squares[:, row, col, :],
+                        in_=lifted[chunk][:, h, j, 1:LIFTED],
+                        func=ACT.Square,
+                        accum_out=norms[chunk][:, j, h : h + 1],
+                    )
+
+        def pool_square(chunk):
+            j0 = POOL_UNIT * BLOCKS
+            vectors = lifted[chunk][:, :, j0 : j0 + BLOCKS, 1:LIFTED].rearrange("p h b d -> p b h d")
+            pool_squares[chunk] = scratch.tile([P, BLOCKS, CHUNK_HEADS, HEAD_DIM], F32, name="pool_sq", tag="pool_sq")
+            nc.gpsimd.tensor_tensor(out=pool_squares[chunk][:], in0=vectors, in1=vectors, op=ALU.mult)
+
+        def vector_norms(chunk):
+            j0 = POOL_UNIT * BLOCKS
+            nc.vector.tensor_reduce(
+                out=norms[chunk][:, j0 : j0 + BLOCKS, :], in_=pool_squares[chunk][:], axis=AXIS.X, op=ALU.add
+            )
+
+        def finish(chunk, heads):
+            h0, h1 = heads[0], heads[-1] + 1
+            nc.scalar.activation(
+                out=lifted[chunk][:, h0:h1, :, 0],
+                in_=norms[chunk][:, :, h0:h1].rearrange("p j h -> p h j"),
+                func=ACT.Sqrt,
+                bias=1.0,
+            )
+            first = (chunk % W_UNITS) * CHUNK_HEADS
+            for b in range(BATCH):
+                nc.sync.dma_start(
+                    out=outputs[chunk // W_UNITS][b, first + h0 : first + h1].rearrange(
+                        "h (p j) c -> p h (j c)", j=J
+                    ),
+                    in_=lifted[chunk][b:P:BATCH, h0:h1].rearrange("p h j c -> p h (j c)"),
+                )
+
+        all_heads = list(range(CHUNK_HEADS))
+        for key in order[0:2]:
+            mx[key] = quantise(flip(raw[key]), key)
+        spread_bias(0)
+        grouped = flip(raw[order[2]], vector_helps=False)
+        flipped, quantised = 3, 2
+
+        for chunk in range(CHUNKS):
+            lifted[chunk] = out_pool.tile([P, CHUNK_HEADS, J, LIFTED], F32, name="lifted", tag="lifted")
+            norms[chunk] = out_pool.tile([P, J, CHUNK_HEADS], F32, name="norms", tag="norms")
+            for unit in range(X_UNITS):
+                if quantised < flipped and (chunk == 0 or unit == 0):
+                    mx[order[quantised]] = quantise(grouped, order[quantised])
+                    quantised += 1
+                if flipped < len(order) and (chunk == 0 or unit == 1):
+                    grouped = flip(raw[order[flipped]])
+                    flipped += 1
+                if chunk == 1 and unit == 0:
+                    spread_bias(1)
+                add_bias(chunk, unit, project(chunk, unit))
+                if unit == POOL_UNIT and chunk > 0:
+                    pool_square(chunk)
+                elif chunk + 1 < CHUNKS or unit + 1 < X_UNITS:
+                    scalar_norms(chunk, all_heads, list(range(unit * BLOCKS, (unit + 1) * BLOCKS)))
+            if chunk > 0:
+                vector_norms(chunk)
+            if chunk + 1 < CHUNKS:
+                finish(chunk, all_heads)
+
+        for h in all_heads:
+            scalar_norms(CHUNKS - 1, [h], list(range(J - BLOCKS, J)))
+            finish(CHUNKS - 1, [h])

@@ -28,9 +28,9 @@ X_UNITS = J // BLOCKS
 CHUNK_HEADS = UNIT_ROWS // HEAD_DIM
 W_UNITS = FEATURES // UNIT_ROWS
 CHUNKS = 2 * W_UNITS
-POOL_UNIT = 0
-STEPS = CHUNKS * X_UNITS
 BANK = 512
+TAIL_CHUNKS = 2
+WARM_MATMULS = 3
 
 FLOPS = 2 * BATCH * TOKENS * K * 2 * FEATURES
 
@@ -52,150 +52,200 @@ def tile_lorentzmultiheadattention_pa_kernel(tc, x_space, Wq, bq, Wk, bk, out_0,
         acc_psum = ctx.enter_context(tc.psum_pool(name="acc", bufs=4))
         ctx.enter_context(tc.manual_schedule())
 
+        zeros = consts.tile([P, BANK], BF16)
+        nc.vector.memset(zeros[:], 0.0)
+        ones = consts.tile([P, P], BF16)
+        nc.vector.memset(ones[:], 1.0)
         one = consts.tile([P, 1], F32)
         nc.vector.memset(one[:], 1.0)
         root = consts.tile([P, 1], F32)
         nc.scalar.activation(out=root[:], in_=one[:], func=ACT.Sqrt)
         ident = consts.tile([P, P], F32)
         make_identity(nc, ident[:])
-        ones = consts.tile([P, P], BF16)
-        nc.vector.memset(ones[:], 1.0)
-        bias_rows = consts.tile([P, 2, FEATURES], BF16)
-        nc.vector.memset(bias_rows[:], 0.0)
+        bias_rows = [consts.tile([P, FEATURES], BF16, name="bias_rows%d" % w) for w in range(2)]
+        nc.vector.memset(bias_rows[0][:], 0.0)
+        nc.gpsimd.memset(bias_rows[1][:], 0.0)
 
-        def load_x(unit):
+        def load_x(unit, pieces):
             raw = raw_pool.tile([P, BLOCKS * K], BF16, name="raw_x%d" % unit)
-            for b in range(BATCH):
-                rows = x_space[b].rearrange("(p j) k -> p (j k)", j=J)
+            width = BLOCKS * K // pieces
+            for piece in range(pieces):
+                for b in range(BATCH):
+                    rows = x_space[b].rearrange("(p j) k -> p (j k)", j=J)
+                    first = unit * BLOCKS * K + piece * width
+                    nc.sync.dma_start(
+                        out=raw[b:P:BATCH, piece * width : (piece + 1) * width],
+                        in_=rows[:, first : first + width],
+                    )
+            return raw
+
+        def load_w(chunk, pieces):
+            raw = raw_pool.tile([P, BLOCKS * K], BF16, name="raw_w%d" % chunk)
+            rows = weights[chunk // W_UNITS].rearrange("(c b r) k -> c r b k", b=BLOCKS, r=P)
+            blocks = BLOCKS // pieces
+            for piece in range(pieces):
                 nc.sync.dma_start(
-                    out=raw[b:P:BATCH, :],
-                    in_=rows[:, unit * BLOCKS * K : (unit + 1) * BLOCKS * K],
+                    out=raw[:].rearrange("p (b k) -> p b k", b=BLOCKS)[:, piece * blocks : (piece + 1) * blocks, :],
+                    in_=rows[chunk % W_UNITS][:, piece * blocks : (piece + 1) * blocks, :],
                 )
             return raw
 
-        def load_w(chunk):
-            raw = raw_pool.tile([P, BLOCKS * K], BF16, name="raw_w%d" % chunk)
-            rows = weights[chunk // W_UNITS].rearrange("(c b r) k -> c r b k", b=BLOCKS, r=P)
-            nc.sync.dma_start(
-                out=raw[:].rearrange("p (b k) -> p b k", b=BLOCKS),
-                in_=rows[chunk % W_UNITS],
-            )
-            return raw
-
-        order = [("x", 0), ("w", 0)]
-        order.extend([("x", unit) for unit in range(1, X_UNITS)])
+        order = [("w", 0)]
+        order.extend([("x", unit) for unit in range(X_UNITS)])
         order.extend([("w", chunk) for chunk in range(1, CHUNKS)])
         raw = {}
-        for kind, n in order:
-            raw[(kind, n)] = load_x(n) if kind == "x" else load_w(n)
-            if (kind, n) == ("w", 0):
+        for place, (kind, n) in enumerate(order):
+            pieces = BLOCKS if place == 0 else 1
+            raw[(kind, n)] = load_x(n, pieces) if kind == "x" else load_w(n, pieces)
+            if place == 2:
                 for w in range(2):
-                    nc.sync.dma_start(out=bias_rows[0:1, w, :], in_=biases[w].unsqueeze(0))
+                    nc.sync.dma_start(out=bias_rows[w][0:1, :], in_=biases[w].unsqueeze(0))
 
-        def flip(raw, vector_helps=True):
-            words = raw[:].bitcast(F32)
-            grouped = stage.tile([P, PASSES * UNIT_ROWS * PACK], BF16, align_bytes=64, tag="grouped")
-            grouped_words = grouped[:].bitcast(F32).rearrange(
-                "p (g b r u) -> p g b r u", g=PASSES, b=BLOCKS, u=HALVES
-            )
-            for b in range(BLOCKS):
-                flipped = flip_psum.tile([P, PASSES, HALVES, P], F32, tag="flip")
+        def warm_up():
+            idle = acc_psum.tile([P, BANK], F32, name="idle", tag="acc")
+            for n in range(WARM_MATMULS):
+                nc.tensor.matmul(out=idle[:], lhsT=ones[:], rhs=zeros[:], start=True, stop=True)
+
+        grouped = {}
+        flipped = {}
+
+        def transpose(key, blocks=(0, 1)):
+            words = raw[key][:].bitcast(F32)
+            for b in blocks:
+                bank = flip_psum.tile([P, PASSES, HALVES, P], F32, name="flipped", tag="flip")
                 for g in range(PASSES):
                     for u in range(HALVES):
                         first = b * ROW_WORDS + g * HALVES * P + u
                         nc.tensor.transpose(
-                            flipped[:, g, u, :], words[:, first : first + HALVES * P - 1 : HALVES], ident[:]
+                            bank[:, g, u, :], words[:, first : first + HALVES * P - 1 : HALVES], ident[:]
                         )
-                source = flipped[:].rearrange("p g u r -> p g r u")
-                if b == 1 and vector_helps:
-                    nc.vector.tensor_copy(out=grouped_words[:, :, b, :, :], in_=source)
-                else:
-                    nc.scalar.copy(out=grouped_words[:, :, b, :, :], in_=source)
-            return grouped
+                flipped[(key, b)] = bank
 
-        def quantise(grouped, key):
-            name = "%s%d" % key
-            codes = mx_pool.tile([P, PASSES, UNIT_ROWS], U32, align_bytes=64, name="codes_" + name)
-            scales = mx_pool.tile([P, PASSES, UNIT_ROWS], U8, align_bytes=64, name="scales_" + name)
-            nc.vector.quantize_mx(
-                out=codes[:].rearrange("p g r -> p (g r)").bitcast(FP8X4),
-                scales=scales[:].rearrange("p g r -> p (g r)"),
-                in_=grouped[:],
-            )
-            return codes, scales
-
-        bias = consts.tile([P, 2, FEATURES], BF16)
-
-        def spread_bias(w):
-            spread = acc_psum.tile([P, FEATURES], BF16, tag="acc")
-            for q in range(FEATURES // BANK):
-                cols = slice(q * BANK, (q + 1) * BANK)
-                nc.tensor.matmul(
-                    out=spread[:, cols], lhsT=ones[:], rhs=bias_rows[:, w, cols], start=True, stop=True
-                )
-            nc.scalar.copy(out=bias[:, w, :], in_=spread[:])
+        def gather(key, b, engine):
+            if key not in grouped:
+                grouped[key] = stage.tile([P, BLOCKS * PASSES * P * PACK], BF16, align_bytes=64, name="grouped", tag="grouped")
+            words = grouped[key][:].bitcast(F32)
+            source = flipped[(key, b)][:].rearrange("p g u r -> p g r u")
+            if key[0] == "x":
+                target = words.rearrange("p (b g r u) -> p b g r u", b=BLOCKS, g=PASSES, u=HALVES)[:, b]
+            else:
+                target = words.rearrange("p (g b r u) -> p g b r u", g=PASSES, b=BLOCKS, u=HALVES)[:, :, b]
+            if engine == "vector":
+                nc.vector.tensor_copy(out=target, in_=source)
+            else:
+                nc.scalar.copy(out=target, in_=source)
 
         mx = {}
-        lifted = [None] * CHUNKS
-        norms = [None] * CHUNKS
-        pool_squares = [None] * CHUNKS
 
-        def project(chunk, unit):
+        def quantise(key, pieces=1):
+            words = BLOCKS * PASSES * P
+            name = "%s%d" % key
+            codes = mx_pool.tile([P, words], U32, align_bytes=64, name="codes_" + name)
+            scales = mx_pool.tile([P, words], U8, align_bytes=64, name="scales_" + name)
+            for piece in range(pieces):
+                part = slice(piece * words // pieces, (piece + 1) * words // pieces)
+                part4 = slice(piece * words * PACK // pieces, (piece + 1) * words * PACK // pieces)
+                nc.vector.quantize_mx(
+                    out=codes[:, part].bitcast(FP8X4), scales=scales[:, part], in_=grouped[key][:, part4]
+                )
+            mx[key] = (codes, scales)
+
+        bias = consts.tile([P, 2, FEATURES], BF16)
+        spread = {}
+
+        def spread_bias(w):
+            bank = acc_psum.tile([P, FEATURES], BF16, name="spread", tag="acc")
+            for q in range(FEATURES // BANK):
+                cols = slice(q * BANK, (q + 1) * BANK)
+                nc.tensor.matmul(out=bank[:, cols], lhsT=ones[:], rhs=bias_rows[w][:, cols], start=True, stop=True)
+            nc.scalar.copy(out=bias[:, w, :], in_=bank[:])
+
+        lifted = {}
+        norms = {}
+        pool_squares = {}
+        acc = {}
+
+        def open_chunk(chunk):
+            lifted[chunk] = out_pool.tile([P, CHUNK_HEADS, J, LIFTED], F32, name="lifted", tag="lifted")
+            norms[chunk] = out_pool.tile([P, J, CHUNK_HEADS], F32, name="norms", tag="norms")
+
+        def project(chunk, unit, h0=0, h1=CHUNK_HEADS):
             x_codes, x_scales = mx[("x", unit)]
             w_codes, w_scales = mx[("w", chunk)]
-            acc = acc_psum.tile([P, BLOCKS, UNIT_ROWS], F32, tag="acc")
+            bank = acc_psum.tile([P, BLOCKS, (h1 - h0) * HEAD_DIM], F32, name="acc", tag="acc")
             for b in range(BLOCKS):
-                tokens = slice(b * P, (b + 1) * P)
                 for g in range(PASSES):
+                    tokens = slice((b * PASSES + g) * P, (b * PASSES + g + 1) * P)
+                    features = slice(g * UNIT_ROWS + h0 * HEAD_DIM, g * UNIT_ROWS + h1 * HEAD_DIM)
                     nc.tensor.matmul_mx(
-                        out=acc[:, b, :],
-                        lhsT=x_codes[:, g, tokens].bitcast(FP8X4),
-                        lhsT_scale=x_scales[:, g, tokens],
-                        rhs=w_codes[:, g, :].bitcast(FP8X4),
-                        rhs_scale=w_scales[:, g, :],
+                        out=bank[:, b, :],
+                        lhsT=x_codes[:, tokens].bitcast(FP8X4),
+                        lhsT_scale=x_scales[:, tokens],
+                        rhs=w_codes[:, features].bitcast(FP8X4),
+                        rhs_scale=w_scales[:, features],
                         start=(g == 0),
                         stop=(g == PASSES - 1),
                     )
-            return acc
+            acc[(chunk, unit)] = bank
 
-        def add_bias(chunk, unit, acc):
+        def add_bias(chunk, unit, h0=0, h1=CHUNK_HEADS):
             first = (chunk % W_UNITS) * UNIT_ROWS
-            bias_chunk = bias[:, chunk // W_UNITS, first : first + UNIT_ROWS].rearrange(
+            bias_chunk = bias[:, chunk // W_UNITS, first + h0 * HEAD_DIM : first + h1 * HEAD_DIM].rearrange(
                 "p (h d) -> p h d", d=HEAD_DIM
             )
             j0 = unit * BLOCKS
             nc.vector.tensor_tensor(
-                out=lifted[chunk][:, :, j0 : j0 + BLOCKS, 1:LIFTED],
-                in0=acc[:].rearrange("p b (h d) -> p h b d", d=HEAD_DIM),
-                in1=bias_chunk.unsqueeze(2).to_broadcast([P, CHUNK_HEADS, BLOCKS, HEAD_DIM]),
+                out=lifted[chunk][:, h0:h1, j0 : j0 + BLOCKS, 1:LIFTED],
+                in0=acc[(chunk, unit)][:].rearrange("p b (h d) -> p h b d", d=HEAD_DIM),
+                in1=bias_chunk.unsqueeze(2).to_broadcast([P, h1 - h0, BLOCKS, HEAD_DIM]),
                 op=ALU.add,
             )
 
-        def scalar_norms(chunk, heads, tokens):
-            squares = scratch.tile([P, len(heads), len(tokens), HEAD_DIM], F32, tag="squares")
-            for row, h in enumerate(heads):
-                for col, j in enumerate(tokens):
+        def vectors_of(chunk, unit, h0=0, h1=CHUNK_HEADS):
+            j0 = unit * BLOCKS
+            return lifted[chunk][:, h0:h1, j0 : j0 + BLOCKS, 1:LIFTED].rearrange("p h b d -> p b h d")
+
+        def scalar_norms(chunk, unit, heads):
+            squares = scratch.tile([P, CHUNK_HEADS, BLOCKS, HEAD_DIM], F32, name="squares", tag="squares")
+            for h in heads:
+                for col in range(BLOCKS):
+                    j = unit * BLOCKS + col
                     nc.scalar.activation(
-                        out=squares[:, row, col, :],
+                        out=squares[:, h, col, :],
                         in_=lifted[chunk][:, h, j, 1:LIFTED],
                         func=ACT.Square,
                         accum_out=norms[chunk][:, j, h : h + 1],
                     )
 
-        def pool_square(chunk):
-            j0 = POOL_UNIT * BLOCKS
-            vectors = lifted[chunk][:, :, j0 : j0 + BLOCKS, 1:LIFTED].rearrange("p h b d -> p b h d")
-            pool_squares[chunk] = scratch.tile([P, BLOCKS, CHUNK_HEADS, HEAD_DIM], F32, name="pool_sq", tag="pool_sq")
-            nc.gpsimd.tensor_tensor(out=pool_squares[chunk][:], in0=vectors, in1=vectors, op=ALU.mult)
+        def pool_square(chunk, unit, h0=0, h1=CHUNK_HEADS):
+            vectors = vectors_of(chunk, unit, h0, h1)
+            squares = scratch.tile([P, BLOCKS, h1 - h0, HEAD_DIM], F32, name="pool_sq", tag="pool_sq")
+            nc.gpsimd.tensor_tensor(out=squares[:], in0=vectors, in1=vectors, op=ALU.mult)
+            halves = scratch.tile([P, BLOCKS, h1 - h0, HEAD_DIM // 2], F32, name="pool_half", tag="pool_half")
+            nc.gpsimd.tensor_tensor(
+                out=halves[:],
+                in0=squares[:, :, :, 0 : HEAD_DIM // 2],
+                in1=squares[:, :, :, HEAD_DIM // 2 : HEAD_DIM],
+                op=ALU.add,
+            )
+            pool_squares[(chunk, unit, h0)] = halves
 
-        def vector_norms(chunk):
-            j0 = POOL_UNIT * BLOCKS
+        def vector_sums(chunk, unit, h0=0, h1=CHUNK_HEADS):
+            j0 = unit * BLOCKS
             nc.vector.tensor_reduce(
-                out=norms[chunk][:, j0 : j0 + BLOCKS, :], in_=pool_squares[chunk][:], axis=AXIS.X, op=ALU.add
+                out=norms[chunk][:, j0 : j0 + BLOCKS, h0:h1], in_=pool_squares[(chunk, unit, h0)][:], axis=AXIS.X, op=ALU.add
             )
 
-        def finish(chunk, heads):
-            h0, h1 = heads[0], heads[-1] + 1
+        def vector_norms(chunk, unit, h0, h1):
+            vectors = vectors_of(chunk, unit, h0, h1)
+            squares = scratch.tile([P, BLOCKS, h1 - h0, HEAD_DIM], F32, name="vector_sq", tag="vector_sq")
+            nc.vector.tensor_tensor(out=squares[:], in0=vectors, in1=vectors, op=ALU.mult)
+            j0 = unit * BLOCKS
+            nc.vector.tensor_reduce(
+                out=norms[chunk][:, j0 : j0 + BLOCKS, h0:h1], in_=squares[:], axis=AXIS.X, op=ALU.add
+            )
+
+        def finish(chunk, h0, h1, pieces=1):
             nc.scalar.activation(
                 out=lifted[chunk][:, h0:h1, :, 0],
                 in_=norms[chunk][:, :, h0:h1].rearrange("p j h -> p h j"),
@@ -203,43 +253,93 @@ def tile_lorentzmultiheadattention_pa_kernel(tc, x_space, Wq, bq, Wk, bk, out_0,
                 bias=1.0,
             )
             first = (chunk % W_UNITS) * CHUNK_HEADS
-            for b in range(BATCH):
-                nc.sync.dma_start(
-                    out=outputs[chunk // W_UNITS][b, first + h0 : first + h1].rearrange(
-                        "h (p j) c -> p h (j c)", j=J
-                    ),
-                    in_=lifted[chunk][b:P:BATCH, h0:h1].rearrange("p h j c -> p h (j c)"),
-                )
+            heads = (h1 - h0) // pieces
+            for piece in range(pieces):
+                low = h0 + piece * heads
+                for b in range(BATCH):
+                    nc.sync.dma_start(
+                        out=outputs[chunk // W_UNITS][b, first + low : first + low + heads].rearrange(
+                            "h (p j) c -> p h (j c)", j=J
+                        ),
+                        in_=lifted[chunk][b:P:BATCH, low : low + heads].rearrange("p h j c -> p h (j c)"),
+                    )
 
-        all_heads = list(range(CHUNK_HEADS))
-        for key in order[0:2]:
-            mx[key] = quantise(flip(raw[key]), key)
+        def pool_units(chunk):
+            if chunk in (0, 2, 4):
+                return (0, 2)
+            return (0,)
+
+        all_heads = range(CHUNK_HEADS)
+        half = CHUNK_HEADS // 2
+
+        warm_up()
+        transpose(("w", 0))
+        gather(("w", 0), 0, "scalar")
+        gather(("w", 0), 1, "vector")
+        transpose(("x", 0))
+        gather(("x", 0), 0, "scalar")
+        gather(("x", 0), 1, "scalar")
+        quantise(("w", 0))
+        quantise(("x", 0), pieces=BLOCKS)
+        transpose(("x", 1))
+        gather(("x", 1), 0, "vector")
+        gather(("x", 1), 1, "scalar")
         spread_bias(0)
-        grouped = flip(raw[order[2]], vector_helps=False)
-        flipped, quantised = 3, 2
 
-        for chunk in range(CHUNKS):
-            lifted[chunk] = out_pool.tile([P, CHUNK_HEADS, J, LIFTED], F32, name="lifted", tag="lifted")
-            norms[chunk] = out_pool.tile([P, J, CHUNK_HEADS], F32, name="norms", tag="norms")
+        for chunk in range(CHUNKS - TAIL_CHUNKS):
+            open_chunk(chunk)
             for unit in range(X_UNITS):
-                if quantised < flipped and (chunk == 0 or unit == 0):
-                    mx[order[quantised]] = quantise(grouped, order[quantised])
-                    quantised += 1
-                if flipped < len(order) and (chunk == 0 or unit == 1):
-                    grouped = flip(raw[order[flipped]])
-                    flipped += 1
-                if chunk == 1 and unit == 0:
+                if chunk == 0:
+                    project(chunk, unit)
+                    quantise(order[unit + 2])
+                    ahead = order[unit + 3]
+                    transpose(ahead)
+                    gather(ahead, 0, "vector" if unit % 2 == 0 else "scalar")
+                    gather(ahead, 1, "scalar")
+                    add_bias(chunk, unit)
+                else:
+                    if unit == 0:
+                        quantise(("w", chunk + 1))
+                    if unit == 1:
+                        transpose(("w", chunk + 2))
+                        gather(("w", chunk + 2), 0, "vector" if chunk % 2 == 0 else "scalar")
+                    project(chunk, unit)
+                    add_bias(chunk, unit)
+                    if unit == 1:
+                        gather(("w", chunk + 2), 1, "scalar")
+                if chunk == 1 and unit == 1:
                     spread_bias(1)
-                add_bias(chunk, unit, project(chunk, unit))
-                if unit == POOL_UNIT and chunk > 0:
-                    pool_square(chunk)
-                elif chunk + 1 < CHUNKS or unit + 1 < X_UNITS:
-                    scalar_norms(chunk, all_heads, list(range(unit * BLOCKS, (unit + 1) * BLOCKS)))
-            if chunk > 0:
-                vector_norms(chunk)
-            if chunk + 1 < CHUNKS:
-                finish(chunk, all_heads)
+                if chunk > 0 and unit in pool_units(chunk - 1):
+                    vector_sums(chunk - 1, unit)
+                    if unit == pool_units(chunk - 1)[-1]:
+                        finish(chunk - 1, 0, CHUNK_HEADS)
+                if unit in pool_units(chunk):
+                    pool_square(chunk, unit)
+                else:
+                    scalar_norms(chunk, unit, all_heads)
 
-        for h in all_heads:
-            scalar_norms(CHUNKS - 1, [h], list(range(J - BLOCKS, J)))
-            finish(CHUNKS - 1, [h])
+        parts = [(chunk, h0) for chunk in range(CHUNKS - TAIL_CHUNKS, CHUNKS) for h0 in (0, half)]
+        for place, (chunk, h0) in enumerate(parts):
+            h1 = h0 + half
+            if h0 == 0:
+                open_chunk(chunk)
+                if chunk + 1 < CHUNKS:
+                    quantise(("w", chunk + 1))
+            final = place + 1 == len(parts)
+            for unit in range(X_UNITS):
+                project(chunk, unit, h0, h1)
+                add_bias(chunk, unit, h0, h1)
+                if place == 0 and unit in pool_units(chunk - 1):
+                    vector_sums(chunk - 1, unit)
+                    if unit == pool_units(chunk - 1)[-1]:
+                        finish(chunk - 1, 0, CHUNK_HEADS)
+                if place > 0 and unit == 3:
+                    vector_sums(parts[place - 1][0], 0, parts[place - 1][1], parts[place - 1][1] + half)
+                    finish(parts[place - 1][0], parts[place - 1][1], parts[place - 1][1] + half)
+                if unit == 0 and not final:
+                    pool_square(chunk, unit, h0, h1)
+                elif not final or unit < 2:
+                    scalar_norms(chunk, unit, range(h0, h1))
+        vector_norms(chunk, 2, h0, h1)
+        vector_norms(chunk, 3, h0, h1)
+        finish(chunk, h0, h1, pieces=half)

@@ -217,10 +217,13 @@ def tile_lorentzmultiheadattention_pa_kernel(tc, x_space, Wq, bq, Wk, bk, out_0,
                         accum_out=norms[chunk][:, j, h : h + 1],
                     )
 
-        def pool_square(chunk, unit, h0=0, h1=CHUNK_HEADS):
+        def pool_square(chunk, unit, h0=0, h1=CHUNK_HEADS, fold=True):
             vectors = vectors_of(chunk, unit, h0, h1)
             squares = scratch.tile([P, BLOCKS, h1 - h0, HEAD_DIM], F32, name="pool_sq", tag="pool_sq")
             nc.gpsimd.tensor_tensor(out=squares[:], in0=vectors, in1=vectors, op=ALU.mult)
+            pool_squares[(chunk, unit, h0)] = squares
+            if not fold:
+                return
             halves = scratch.tile([P, BLOCKS, h1 - h0, HEAD_DIM // 2], F32, name="pool_half", tag="pool_half")
             nc.gpsimd.tensor_tensor(
                 out=halves[:],
@@ -236,14 +239,11 @@ def tile_lorentzmultiheadattention_pa_kernel(tc, x_space, Wq, bq, Wk, bk, out_0,
                 out=norms[chunk][:, j0 : j0 + BLOCKS, h0:h1], in_=pool_squares[(chunk, unit, h0)][:], axis=AXIS.X, op=ALU.add
             )
 
-        def vector_norms(chunk, unit, h0, h1):
+        def vector_squares(chunk, unit, h0, h1):
             vectors = vectors_of(chunk, unit, h0, h1)
             squares = scratch.tile([P, BLOCKS, h1 - h0, HEAD_DIM], F32, name="vector_sq", tag="vector_sq")
             nc.vector.tensor_tensor(out=squares[:], in0=vectors, in1=vectors, op=ALU.mult)
-            j0 = unit * BLOCKS
-            nc.vector.tensor_reduce(
-                out=norms[chunk][:, j0 : j0 + BLOCKS, h0:h1], in_=squares[:], axis=AXIS.X, op=ALU.add
-            )
+            pool_squares[(chunk, unit, h0)] = squares
 
         def finish(chunk, h0, h1, pieces=1):
             nc.scalar.activation(
@@ -264,82 +264,72 @@ def tile_lorentzmultiheadattention_pa_kernel(tc, x_space, Wq, bq, Wk, bk, out_0,
                         in_=lifted[chunk][b:P:BATCH, low : low + heads].rearrange("p h j c -> p h (j c)"),
                     )
 
-        def pool_units(chunk):
-            if chunk in (0, 2, 4):
-                return (0, 2)
-            return (0,)
-
-        all_heads = range(CHUNK_HEADS)
         half = CHUNK_HEADS // 2
+        whole = CHUNKS - TAIL_CHUNKS
+        parts = [(chunk, 0, CHUNK_HEADS) for chunk in range(whole)]
+        parts.extend([(chunk, h0, h0 + half) for chunk in range(whole, CHUNKS) for h0 in (0, half)])
+        final = len(parts) - 1
+
+        def pool_units(place):
+            if place == 0 or place == final:
+                return ()
+            return (0,) if place < whole else (0, 1)
+
+        def close(place, unit):
+            before, h0, h1 = parts[place - 1]
+            units = pool_units(place - 1)
+            if unit in units:
+                vector_sums(before, unit, h0, h1)
+            if unit == max(units, default=0):
+                finish(before, h0, h1)
 
         warm_up()
-        transpose(("w", 0))
-        gather(("w", 0), 0, "scalar")
-        gather(("w", 0), 1, "vector")
-        transpose(("x", 0))
-        gather(("x", 0), 0, "scalar")
-        gather(("x", 0), 1, "scalar")
-        quantise(("w", 0))
-        quantise(("x", 0), pieces=BLOCKS)
-        transpose(("x", 1))
-        gather(("x", 1), 0, "vector")
-        gather(("x", 1), 1, "scalar")
+        transpose(order[0])
+        gather(order[0], 0, "scalar")
+        gather(order[0], 1, "vector")
+        transpose(order[1])
+        gather(order[1], 0, "scalar")
+        gather(order[1], 1, "scalar")
+        quantise(order[0])
+        quantise(order[1], pieces=BLOCKS)
+        transpose(order[2])
+        gather(order[2], 0, "vector")
+        gather(order[2], 1, "scalar")
         spread_bias(0)
 
-        for chunk in range(CHUNKS - TAIL_CHUNKS):
-            open_chunk(chunk)
-            for unit in range(X_UNITS):
-                if chunk == 0:
-                    project(chunk, unit)
-                    quantise(order[unit + 2])
-                    ahead = order[unit + 3]
-                    transpose(ahead)
-                    gather(ahead, 0, "vector" if unit % 2 == 0 else "scalar")
-                    gather(ahead, 1, "scalar")
-                    add_bias(chunk, unit)
-                else:
-                    if unit == 0:
-                        quantise(("w", chunk + 1))
-                    if unit == 1:
-                        transpose(("w", chunk + 2))
-                        gather(("w", chunk + 2), 0, "vector" if chunk % 2 == 0 else "scalar")
-                    project(chunk, unit)
-                    add_bias(chunk, unit)
-                    if unit == 1:
-                        gather(("w", chunk + 2), 1, "scalar")
-                if chunk == 1 and unit == 1:
-                    spread_bias(1)
-                if chunk > 0 and unit in pool_units(chunk - 1):
-                    vector_sums(chunk - 1, unit)
-                    if unit == pool_units(chunk - 1)[-1]:
-                        finish(chunk - 1, 0, CHUNK_HEADS)
-                if unit in pool_units(chunk):
-                    pool_square(chunk, unit)
-                else:
-                    scalar_norms(chunk, unit, all_heads)
-
-        parts = [(chunk, h0) for chunk in range(CHUNKS - TAIL_CHUNKS, CHUNKS) for h0 in (0, half)]
-        for place, (chunk, h0) in enumerate(parts):
-            h1 = h0 + half
+        for place, (chunk, h0, h1) in enumerate(parts):
             if h0 == 0:
                 open_chunk(chunk)
-                if chunk + 1 < CHUNKS:
-                    quantise(("w", chunk + 1))
-            final = place + 1 == len(parts)
             for unit in range(X_UNITS):
+                ready, ahead, helper = None, None, "vector"
+                if chunk == 0:
+                    ready, ahead = order[unit + 2], order[unit + 3]
+                    helper = "vector" if unit % 2 == 0 else "scalar"
+                elif h0 == 0 and unit == 0 and chunk + 1 < CHUNKS:
+                    ready = ("w", chunk + 1)
+                elif h0 == 0 and unit == 1 and chunk + 2 < CHUNKS:
+                    ahead = ("w", chunk + 2)
+                if ready:
+                    quantise(ready)
+                if ahead:
+                    transpose(ahead)
+                    if helper == "vector":
+                        gather(ahead, 0, "vector")
                 project(chunk, unit, h0, h1)
                 add_bias(chunk, unit, h0, h1)
-                if place == 0 and unit in pool_units(chunk - 1):
-                    vector_sums(chunk - 1, unit)
-                    if unit == pool_units(chunk - 1)[-1]:
-                        finish(chunk - 1, 0, CHUNK_HEADS)
-                if place > 0 and unit == 3:
-                    vector_sums(parts[place - 1][0], 0, parts[place - 1][1], parts[place - 1][1] + half)
-                    finish(parts[place - 1][0], parts[place - 1][1], parts[place - 1][1] + half)
-                if unit == 0 and not final:
-                    pool_square(chunk, unit, h0, h1)
-                elif not final or unit < 2:
+                if ahead:
+                    if helper == "scalar":
+                        gather(ahead, 0, "scalar")
+                    gather(ahead, 1, "scalar")
+                if (chunk, unit) == (1, 1):
+                    spread_bias(1)
+                if place > 0:
+                    close(place, unit)
+                if unit in pool_units(place):
+                    pool_square(chunk, unit, h0, h1, fold=place < whole)
+                elif place < final or unit < X_UNITS - 1:
                     scalar_norms(chunk, unit, range(h0, h1))
-        vector_norms(chunk, 2, h0, h1)
-        vector_norms(chunk, 3, h0, h1)
+
+        vector_squares(chunk, X_UNITS - 1, h0, h1)
+        vector_sums(chunk, X_UNITS - 1, h0, h1)
         finish(chunk, h0, h1, pieces=half)

@@ -62,9 +62,8 @@ def tile_lorentzmultiheadattention_pa_kernel(tc, x_space, Wq, bq, Wk, bk, out_0,
         nc.scalar.activation(out=root[:], in_=one[:], func=ACT.Sqrt)
         ident = consts.tile([P, P], F32)
         make_identity(nc, ident[:])
-        bias_rows = [consts.tile([P, FEATURES], BF16, name="bias_rows%d" % w) for w in range(2)]
+        bias_rows = [consts.tile([P, FEATURES], BF16, name="bias_rows%d" % w) for w in range(1)]
         nc.vector.memset(bias_rows[0][:], 0.0)
-        nc.gpsimd.memset(bias_rows[1][:], 0.0)
 
         def load_x(unit, pieces):
             raw = raw_pool.tile([P, BLOCKS * K], BF16, name="raw_x%d" % unit)
@@ -98,8 +97,9 @@ def tile_lorentzmultiheadattention_pa_kernel(tc, x_space, Wq, bq, Wk, bk, out_0,
             pieces = BLOCKS if place == 0 else 1
             raw[(kind, n)] = load_x(n, pieces) if kind == "x" else load_w(n, pieces)
             if place == 2:
-                for w in range(2):
-                    nc.sync.dma_start(out=bias_rows[w][0:1, :], in_=biases[w].unsqueeze(0))
+                nc.sync.dma_start(out=bias_rows[0][0:1, :], in_=biases[0].unsqueeze(0))
+        bias = consts.tile([P, 2, FEATURES], BF16)
+        nc.sync.dma_start(out=bias[:, 1, :], in_=biases[1].partition_broadcast(P))
 
         def warm_up():
             idle = acc_psum.tile([P, BANK], F32, name="idle", tag="acc")
@@ -150,8 +150,6 @@ def tile_lorentzmultiheadattention_pa_kernel(tc, x_space, Wq, bq, Wk, bk, out_0,
                 )
             mx[key] = (codes, scales)
 
-        bias = consts.tile([P, 2, FEATURES], BF16)
-        spread = {}
 
         def spread_bias(w):
             bank = acc_psum.tile([P, FEATURES], BF16, name="spread", tag="acc")
@@ -321,12 +319,15 @@ def tile_lorentzmultiheadattention_pa_kernel(tc, x_space, Wq, bq, Wk, bk, out_0,
                     if helper == "scalar":
                         gather(ahead, 0, "scalar")
                     gather(ahead, 1, "scalar")
-                if (chunk, unit) == (1, 1):
-                    spread_bias(1)
+                if (place, unit) == (1, 0):
+                    scalar_norms(0, X_UNITS - 1, range(CHUNK_HEADS))
                 if place > 0:
                     close(place, unit)
                 if unit in pool_units(place):
                     pool_square(chunk, unit, h0, h1, fold=place < whole)
+                elif place == 0:
+                    if unit > 0:
+                        scalar_norms(chunk, unit - 1, range(h0, h1))
                 elif place < final or unit < X_UNITS - 1:
                     scalar_norms(chunk, unit, range(h0, h1))
 

@@ -278,7 +278,7 @@ def tile_lorentzmultiheadattention_pa_kernel(tc, x_space, Wq, bq, Wk, bk, out_0,
             units = pool_units(place - 1)
             if unit in units:
                 vector_sums(before, unit, h0, h1)
-            if unit == max(units, default=0):
+            if unit == 1:
                 finish(before, h0, h1)
 
         warm_up()

@@ -307,7 +307,7 @@ def tile_lorentzmultiheadattention_pa_kernel(tc, x_space, Wq, bq, Wk, bk, out_0,
                     ready = ("w", chunk + 1)
                 elif h0 == 0 and unit == 1 and chunk + 2 < CHUNKS:
                     ahead = ("w", chunk + 2)
-                if ready:
+                if ready and chunk == 0:
                     quantise(ready)
                 if ahead:
                     transpose(ahead)
@@ -315,6 +315,8 @@ def tile_lorentzmultiheadattention_pa_kernel(tc, x_space, Wq, bq, Wk, bk, out_0,
                         gather(ahead, 0, "vector")
                 project(chunk, unit, h0, h1)
                 add_bias(chunk, unit, h0, h1)
+                if ready and chunk > 0:
+                    quantise(ready)
                 if ahead:
                     if helper == "scalar":
                         gather(ahead, 0, "scalar")

@@ -96,7 +96,7 @@ def tile_lorentzmultiheadattention_pa_kernel(tc, x_space, Wq, bq, Wk, bk, out_0,
         for place, (kind, n) in enumerate(order):
             pieces = BLOCKS if place == 0 else 1
             raw[(kind, n)] = load_x(n, pieces) if kind == "x" else load_w(n, pieces)
-            if place == 2:
+            if place == 1:
                 nc.sync.dma_start(out=bias_rows[0][0:1, :], in_=biases[0].unsqueeze(0))
         bias = consts.tile([P, 2, FEATURES], BF16)
         nc.sync.dma_start(out=bias[:, 1, :], in_=biases[1].partition_broadcast(P))
@@ -284,43 +284,45 @@ def tile_lorentzmultiheadattention_pa_kernel(tc, x_space, Wq, bq, Wk, bk, out_0,
         warm_up()
         transpose(order[0])
         gather(order[0], 0, "scalar")
-        gather(order[0], 1, "vector")
         transpose(order[1])
-        gather(order[1], 0, "scalar")
-        gather(order[1], 1, "scalar")
+        gather(order[0], 1, "vector")
         quantise(order[0])
-        quantise(order[1], pieces=BLOCKS)
+        gather(order[1], 0, "scalar")
+        spread_bias(0)
         transpose(order[2])
+        gather(order[1], 1, "vector")
+        quantise(order[1], pieces=BLOCKS)
+        transpose(order[3])
         gather(order[2], 0, "vector")
         gather(order[2], 1, "scalar")
-        spread_bias(0)
 
         for place, (chunk, h0, h1) in enumerate(parts):
             if h0 == 0:
                 open_chunk(chunk)
             for unit in range(X_UNITS):
-                ready, ahead, helper = None, None, "vector"
                 if chunk == 0:
-                    ready, ahead = order[unit + 2], order[unit + 3]
-                    helper = "vector" if unit % 2 == 0 else "scalar"
-                elif h0 == 0 and unit == 0 and chunk + 1 < CHUNKS:
-                    ready = ("w", chunk + 1)
-                elif h0 == 0 and unit == 1 and chunk + 2 < CHUNKS:
-                    ahead = ("w", chunk + 2)
-                if ready and chunk == 0:
-                    quantise(ready)
-                if ahead:
-                    transpose(ahead)
-                    if helper == "vector":
+                    if unit < X_UNITS - 1:
+                        quantise(order[unit + 2])
+                    project(chunk, unit, h0, h1)
+                    if unit < X_UNITS - 1:
+                        transpose(order[unit + 4])
+                    emptied = order[unit + 3]
+                    gather(emptied, 0, "scalar")
+                    gather(emptied, 1, "vector" if emptied == ("w", 1) else "scalar")
+                    if emptied == ("w", 1):
+                        quantise(emptied)
+                    add_bias(chunk, unit, h0, h1)
+                else:
+                    ahead = ("w", chunk + 2) if h0 == 0 and unit == 1 and chunk + 2 < CHUNKS else None
+                    if ahead:
+                        transpose(ahead)
                         gather(ahead, 0, "vector")
-                project(chunk, unit, h0, h1)
-                add_bias(chunk, unit, h0, h1)
-                if ready and chunk > 0:
-                    quantise(ready)
-                if ahead:
-                    if helper == "scalar":
-                        gather(ahead, 0, "scalar")
-                    gather(ahead, 1, "scalar")
+                    project(chunk, unit, h0, h1)
+                    add_bias(chunk, unit, h0, h1)
+                    if h0 == 0 and unit == 0 and chunk + 1 < CHUNKS:
+                        quantise(("w", chunk + 1))
+                    if ahead:
+                        gather(ahead, 1, "scalar")
                 if (place, unit) == (1, 0):
                     scalar_norms(0, X_UNITS - 1, range(CHUNK_HEADS))
                 if place > 0:

@@ -29,7 +29,7 @@ CHUNK_HEADS = UNIT_ROWS // HEAD_DIM
 W_UNITS = FEATURES // UNIT_ROWS
 CHUNKS = 2 * W_UNITS
 BANK = 512
-TAIL_CHUNKS = 2
+TAIL_CHUNKS = 3
 WARM_MATMULS = 3
 
 FLOPS = 2 * BATCH * TOKENS * K * 2 * FEATURES
@@ -269,9 +269,9 @@ def tile_lorentzmultiheadattention_pa_kernel(tc, x_space, Wq, bq, Wk, bk, out_0,
         final = len(parts) - 1
 
         def pool_units(place):
-            if place == 0 or place == final:
+            if place == 0:
                 return ()
-            return (0,) if place < whole else (0, 1)
+            return (0, 1) if CHUNKS - 2 <= parts[place][0] and place < final else (0,)
 
         def close(place, unit):
             before, h0, h1 = parts[place - 1]
@@ -316,7 +316,7 @@ def tile_lorentzmultiheadattention_pa_kernel(tc, x_space, Wq, bq, Wk, bk, out_0,
                     ahead = ("w", chunk + 2) if h0 == 0 and unit == 1 and chunk + 2 < CHUNKS else None
                     if ahead:
                         transpose(ahead)
-                        gather(ahead, 0, "vector")
+                        gather(ahead, 0, "scalar" if chunk == 2 else "vector")
                     project(chunk, unit, h0, h1)
                     add_bias(chunk, unit, h0, h1)
                     if h0 == 0 and unit == 0 and chunk + 1 < CHUNKS:
@@ -336,5 +336,7 @@ def tile_lorentzmultiheadattention_pa_kernel(tc, x_space, Wq, bq, Wk, bk, out_0,
                     scalar_norms(chunk, unit, range(h0, h1))
 
         vector_squares(chunk, X_UNITS - 1, h0, h1)
+        for unit in pool_units(final):
+            vector_sums(chunk, unit, h0, h1)
         vector_sums(chunk, X_UNITS - 1, h0, h1)
         finish(chunk, h0, h1, pieces=half)

@@ -29,7 +29,7 @@ CHUNK_HEADS = UNIT_ROWS // HEAD_DIM
 W_UNITS = FEATURES // UNIT_ROWS
 CHUNKS = 2 * W_UNITS
 BANK = 512
-TAIL_CHUNKS = 3
+TAIL_CHUNKS = 2
 WARM_MATMULS = 3
 
 FLOPS = 2 * BATCH * TOKENS * K * 2 * FEATURES
@@ -267,6 +267,8 @@ def tile_lorentzmultiheadattention_pa_kernel(tc, x_space, Wq, bq, Wk, bk, out_0,
         parts = [(chunk, 0, CHUNK_HEADS) for chunk in range(whole)]
         parts.extend([(chunk, h0, h0 + half) for chunk in range(whole, CHUNKS) for h0 in (0, half)])
         final = len(parts) - 1
+        by_heads = (whole - 2, whole - 1)
+        late_units = (X_UNITS - 2, X_UNITS - 1)
 
         def pool_units(place):
             if place == 0:
@@ -275,11 +277,14 @@ def tile_lorentzmultiheadattention_pa_kernel(tc, x_space, Wq, bq, Wk, bk, out_0,
 
         def close(place, unit):
             before, h0, h1 = parts[place - 1]
-            units = pool_units(place - 1)
-            if unit in units:
+            if unit in pool_units(place - 1):
                 vector_sums(before, unit, h0, h1)
+            if unit == 0 and place - 1 in by_heads:
+                finish(before, h0, h0 + half)
+                for late in late_units:
+                    scalar_norms(before, late, range(h0 + half, h1))
             if unit == 1:
-                finish(before, h0, h1)
+                finish(before, h0 + half if place - 1 in by_heads else h0, h1)
 
         warm_up()
         transpose(order[0])
@@ -332,6 +337,10 @@ def tile_lorentzmultiheadattention_pa_kernel(tc, x_space, Wq, bq, Wk, bk, out_0,
                 elif place == 0:
                     if unit > 0:
                         scalar_norms(chunk, unit - 1, range(h0, h1))
+                elif place in by_heads and unit in late_units:
+                    if unit == X_UNITS - 1:
+                        for late in late_units:
+                            scalar_norms(chunk, late, range(h0, h0 + half))
                 elif place < final or unit < X_UNITS - 1:
                     scalar_norms(chunk, unit, range(h0, h1))
 

from contextlib import ExitStack

import concourse.mybir as mybir
from concourse.masks import make_identity

F32 = mybir.dt.float32
BF16 = mybir.dt.bfloat16
U32 = mybir.dt.uint32
U8 = mybir.dt.uint8
FP8X4 = mybir.dt.float8_e4m3fn_x4
ACT = mybir.ActivationFunctionType
ALU = mybir.AluOpType
AXIS = mybir.AxisListType

P = 128
BATCH, TOKENS, K = 2, 512, 1024
FEATURES, HEAD_DIM = 1024, 64
LIFTED = HEAD_DIM + 1
PACK = 4
K_PASS = P * PACK
PASSES = K // K_PASS
HALVES = 2
ROW_WORDS = K // 2
BLOCKS = 2
UNIT_ROWS = BLOCKS * P
J = BATCH * TOKENS // P
X_UNITS = J // BLOCKS
CHUNK_HEADS = UNIT_ROWS // HEAD_DIM
W_UNITS = FEATURES // UNIT_ROWS
CHUNKS = 2 * W_UNITS
BANK = 512
TAIL_CHUNKS = 2
WARM_MATMULS = 3

FLOPS = 2 * BATCH * TOKENS * K * 2 * FEATURES


def tile_lorentzmultiheadattention_pa_kernel(tc, x_space, Wq, bq, Wk, bk, out_0, out_1):
    nc = tc.nc
    weights = (Wq, Wk)
    biases = (bq, bk)
    outputs = (out_0, out_1)

    with ExitStack() as ctx:
        consts = ctx.enter_context(tc.tile_pool(name="consts", bufs=1))
        raw_pool = ctx.enter_context(tc.tile_pool(name="raw", bufs=1))
        mx_pool = ctx.enter_context(tc.tile_pool(name="mx", bufs=1))
        stage = ctx.enter_context(tc.tile_pool(name="stage", bufs=4))
        out_pool = ctx.enter_context(tc.tile_pool(name="outp", bufs=CHUNKS))
        scratch = ctx.enter_context(tc.tile_pool(name="scratch", bufs=4))
        flip_psum = ctx.enter_context(tc.psum_pool(name="flip", bufs=4))
        acc_psum = ctx.enter_context(tc.psum_pool(name="acc", bufs=4))
        ctx.enter_context(tc.manual_schedule())

        zeros = consts.tile([P, BANK], BF16)
        nc.vector.memset(zeros[:], 0.0)
        ones = consts.tile([P, P], BF16)
        nc.vector.memset(ones[:], 1.0)
        one = consts.tile([P, 1], F32)
        nc.vector.memset(one[:], 1.0)
        root = consts.tile([P, 1], F32)
        nc.scalar.activation(out=root[:], in_=one[:], func=ACT.Sqrt)
        ident = consts.tile([P, P], F32)
        make_identity(nc, ident[:])
        bias_rows = [consts.tile([P, FEATURES], BF16, name="bias_rows%d" % w) for w in range(1)]
        nc.vector.memset(bias_rows[0][:], 0.0)

        def load_x(unit, pieces):
            raw = raw_pool.tile([P, BLOCKS * K], BF16, name="raw_x%d" % unit)
            width = BLOCKS * K // pieces
            for piece in range(pieces):
                for b in range(BATCH):
                    rows = x_space[b].rearrange("(p j) k -> p (j k)", j=J)
                    first = unit * BLOCKS * K + piece * width
                    nc.sync.dma_start(
                        out=raw[b:P:BATCH, piece * width : (piece + 1) * width],
                        in_=rows[:, first : first + width],
                    )
            return raw

        def load_w(chunk, pieces):
            raw = raw_pool.tile([P, BLOCKS * K], BF16, name="raw_w%d" % chunk)
            rows = weights[chunk // W_UNITS].rearrange("(c b r) k -> c r b k", b=BLOCKS, r=P)
            blocks = BLOCKS // pieces
            for piece in range(pieces):
                nc.sync.dma_start(
                    out=raw[:].rearrange("p (b k) -> p b k", b=BLOCKS)[:, piece * blocks : (piece + 1) * blocks, :],
                    in_=rows[chunk % W_UNITS][:, piece * blocks : (piece + 1) * blocks, :],
                )
            return raw

        order = [("w", 0)]
        order.extend([("x", unit) for unit in range(X_UNITS)])
        order.extend([("w", chunk) for chunk in range(1, CHUNKS)])
        raw = {}
        for place, (kind, n) in enumerate(order):
            pieces = BLOCKS if place == 0 else 1
            raw[(kind, n)] = load_x(n, pieces) if kind == "x" else load_w(n, pieces)
            if place == 1:
                nc.sync.dma_start(out=bias_rows[0][0:1, :], in_=biases[0].unsqueeze(0))
        bias = consts.tile([P, 2, FEATURES], BF16)
        nc.sync.dma_start(out=bias[:, 1, :], in_=biases[1].partition_broadcast(P))

        def warm_up():
            idle = acc_psum.tile([P, BANK], F32, name="idle", tag="acc")
            for n in range(WARM_MATMULS):
                nc.tensor.matmul(out=idle[:], lhsT=ones[:], rhs=zeros[:], start=True, stop=True)

        grouped = {}
        flipped = {}

        def transpose(key, blocks=(0, 1)):
            words = raw[key][:].bitcast(F32)
            for b in blocks:
                bank = flip_psum.tile([P, PASSES, HALVES, P], F32, name="flipped", tag="flip")
                for g in range(PASSES):
                    for u in range(HALVES):
                        first = b * ROW_WORDS + g * HALVES * P + u
                        nc.tensor.transpose(
                            bank[:, g, u, :], words[:, first : first + HALVES * P - 1 : HALVES], ident[:]
                        )
                flipped[(key, b)] = bank

        def gather(key, b, engine):
            if key not in grouped:
                grouped[key] = stage.tile([P, BLOCKS * PASSES * P * PACK], BF16, align_bytes=64, name="grouped", tag="grouped")
            words = grouped[key][:].bitcast(F32)
            source = flipped[(key, b)][:].rearrange("p g u r -> p g r u")
            if key[0] == "x":
                target = words.rearrange("p (b g r u) -> p b g r u", b=BLOCKS, g=PASSES, u=HALVES)[:, b]
            else:
                target = words.rearrange("p (g b r u) -> p g b r u", g=PASSES, b=BLOCKS, u=HALVES)[:, :, b]
            if engine == "vector":
                nc.vector.tensor_copy(out=target, in_=source)
            else:
                nc.scalar.copy(out=target, in_=source)

        mx = {}

        def quantise(key, pieces=1):
            words = BLOCKS * PASSES * P
            name = "%s%d" % key
            codes = mx_pool.tile([P, words], U32, align_bytes=64, name="codes_" + name)
            scales = mx_pool.tile([P, words], U8, align_bytes=64, name="scales_" + name)
            for piece in range(pieces):
                part = slice(piece * words // pieces, (piece + 1) * words // pieces)
                part4 = slice(piece * words * PACK // pieces, (piece + 1) * words * PACK // pieces)
                nc.vector.quantize_mx(
                    out=codes[:, part].bitcast(FP8X4), scales=scales[:, part], in_=grouped[key][:, part4]
                )
            mx[key] = (codes, scales)


        def spread_bias(w):
            bank = acc_psum.tile([P, FEATURES], BF16, name="spread", tag="acc")
            for q in range(FEATURES // BANK):
                cols = slice(q * BANK, (q + 1) * BANK)
                nc.tensor.matmul(out=bank[:, cols], lhsT=ones[:], rhs=bias_rows[w][:, cols], start=True, stop=True)
            nc.scalar.copy(out=bias[:, w, :], in_=bank[:])

        lifted = {}
        norms = {}
        pool_squares = {}
        acc = {}

        def open_chunk(chunk):
            lifted[chunk] = out_pool.tile([P, CHUNK_HEADS, J, LIFTED], F32, name="lifted", tag="lifted")
            norms[chunk] = out_pool.tile([P, J, CHUNK_HEADS], F32, name="norms", tag="norms")

        def project(chunk, unit, h0=0, h1=CHUNK_HEADS):
            x_codes, x_scales = mx[("x", unit)]
            w_codes, w_scales = mx[("w", chunk)]
            bank = acc_psum.tile([P, BLOCKS, (h1 - h0) * HEAD_DIM], F32, name="acc", tag="acc")
            for b in range(BLOCKS):
                for g in range(PASSES):
                    tokens = slice((b * PASSES + g) * P, (b * PASSES + g + 1) * P)
                    features = slice(g * UNIT_ROWS + h0 * HEAD_DIM, g * UNIT_ROWS + h1 * HEAD_DIM)
                    nc.tensor.matmul_mx(
                        out=bank[:, b, :],
                        lhsT=x_codes[:, tokens].bitcast(FP8X4),
                        lhsT_scale=x_scales[:, tokens],
                        rhs=w_codes[:, features].bitcast(FP8X4),
                        rhs_scale=w_scales[:, features],
                        start=(g == 0),
                        stop=(g == PASSES - 1),
                    )
            acc[(chunk, unit)] = bank

        def add_bias(chunk, unit, h0=0, h1=CHUNK_HEADS):
            first = (chunk % W_UNITS) * UNIT_ROWS
            bias_chunk = bias[:, chunk // W_UNITS, first + h0 * HEAD_DIM : first + h1 * HEAD_DIM].rearrange(
                "p (h d) -> p h d", d=HEAD_DIM
            )
            j0 = unit * BLOCKS
            nc.vector.tensor_tensor(
                out=lifted[chunk][:, h0:h1, j0 : j0 + BLOCKS, 1:LIFTED],
                in0=acc[(chunk, unit)][:].rearrange("p b (h d) -> p h b d", d=HEAD_DIM),
                in1=bias_chunk.unsqueeze(2).to_broadcast([P, h1 - h0, BLOCKS, HEAD_DIM]),
                op=ALU.add,
            )

        def vectors_of(chunk, unit, h0=0, h1=CHUNK_HEADS):
            j0 = unit * BLOCKS
            return lifted[chunk][:, h0:h1, j0 : j0 + BLOCKS, 1:LIFTED].rearrange("p h b d -> p b h d")

        def scalar_norms(chunk, unit, heads):
            squares = scratch.tile([P, CHUNK_HEADS, BLOCKS, HEAD_DIM], F32, name="squares", tag="squares")
            for h in heads:
                for col in range(BLOCKS):
                    j = unit * BLOCKS + col
                    nc.scalar.activation(
                        out=squares[:, h, col, :],
                        in_=lifted[chunk][:, h, j, 1:LIFTED],
                        func=ACT.Square,
                        accum_out=norms[chunk][:, j, h : h + 1],
                    )

        def pool_square(chunk, unit, h0=0, h1=CHUNK_HEADS, fold=True):
            vectors = vectors_of(chunk, unit, h0, h1)
            squares = scratch.tile([P, BLOCKS, h1 - h0, HEAD_DIM], F32, name="pool_sq", tag="pool_sq")
            nc.gpsimd.tensor_tensor(out=squares[:], in0=vectors, in1=vectors, op=ALU.mult)
            pool_squares[(chunk, unit, h0)] = squares
            if not fold:
                return
            halves = scratch.tile([P, BLOCKS, h1 - h0, HEAD_DIM // 2], F32, name="pool_half", tag="pool_half")
            nc.gpsimd.tensor_tensor(
                out=halves[:],
                in0=squares[:, :, :, 0 : HEAD_DIM // 2],
                in1=squares[:, :, :, HEAD_DIM // 2 : HEAD_DIM],
                op=ALU.add,
            )
            pool_squares[(chunk, unit, h0)] = halves

        def vector_sums(chunk, unit, h0=0, h1=CHUNK_HEADS):
            j0 = unit * BLOCKS
            nc.vector.tensor_reduce(
                out=norms[chunk][:, j0 : j0 + BLOCKS, h0:h1], in_=pool_squares[(chunk, unit, h0)][:], axis=AXIS.X, op=ALU.add
            )

        def vector_squares(chunk, unit, h0, h1):
            vectors = vectors_of(chunk, unit, h0, h1)
            squares = scratch.tile([P, BLOCKS, h1 - h0, HEAD_DIM], F32, name="vector_sq", tag="vector_sq")
            nc.vector.tensor_tensor(out=squares[:], in0=vectors, in1=vectors, op=ALU.mult)
            pool_squares[(chunk, unit, h0)] = squares

        def finish(chunk, h0, h1, pieces=1):
            nc.scalar.activation(
                out=lifted[chunk][:, h0:h1, :, 0],
                in_=norms[chunk][:, :, h0:h1].rearrange("p j h -> p h j"),
                func=ACT.Sqrt,
                bias=1.0,
            )
            first = (chunk % W_UNITS) * CHUNK_HEADS
            heads = (h1 - h0) // pieces
            for piece in range(pieces):
                low = h0 + piece * heads
                for b in range(BATCH):
                    nc.sync.dma_start(
                        out=outputs[chunk // W_UNITS][b, first + low : first + low + heads].rearrange(
                            "h (p j) c -> p h (j c)", j=J
                        ),
                        in_=lifted[chunk][b:P:BATCH, low : low + heads].rearrange("p h j c -> p h (j c)"),
                    )

        half = CHUNK_HEADS // 2
        whole = CHUNKS - TAIL_CHUNKS
        parts = [(chunk, 0, CHUNK_HEADS) for chunk in range(whole)]
        parts.extend([(chunk, h0, h0 + half) for chunk in range(whole, CHUNKS) for h0 in (0, half)])
        final = len(parts) - 1
        by_heads = (whole - 2, whole - 1)
        late_units = (X_UNITS - 2, X_UNITS - 1)

        def pool_units(place):
            if place == 0:
                return ()
            return (0, 1) if CHUNKS - 2 <= parts[place][0] and place < final else (0,)

        def close(place, unit):
            before, h0, h1 = parts[place - 1]
            if unit in pool_units(place - 1):
                vector_sums(before, unit, h0, h1)
            if unit == 0 and place - 1 in by_heads:
                finish(before, h0, h0 + half)
                for late in late_units:
                    scalar_norms(before, late, range(h0 + half, h1))
            if unit == 1:
                finish(before, h0 + half if place - 1 in by_heads else h0, h1)

        warm_up()
        transpose(order[0])
        gather(order[0], 0, "scalar")
        transpose(order[1])
        gather(order[0], 1, "vector")
        quantise(order[0])
        gather(order[1], 0, "scalar")
        spread_bias(0)
        transpose(order[2])
        gather(order[1], 1, "vector")
        quantise(order[1], pieces=BLOCKS)
        transpose(order[3])
        gather(order[2], 0, "vector")
        gather(order[2], 1, "scalar")

        for place, (chunk, h0, h1) in enumerate(parts):
            if h0 == 0:
                open_chunk(chunk)
            for unit in range(X_UNITS):
                if chunk == 0:
                    if unit < X_UNITS - 1:
                        quantise(order[unit + 2])
                    project(chunk, unit, h0, h1)
                    if unit < X_UNITS - 1:
                        transpose(order[unit + 4])
                    emptied = order[unit + 3]
                    gather(emptied, 0, "scalar")
                    gather(emptied, 1, "vector" if emptied == ("w", 1) else "scalar")
                    if emptied == ("w", 1):
                        quantise(emptied)
                    add_bias(chunk, unit, h0, h1)
                else:
                    ahead = ("w", chunk + 2) if h0 == 0 and unit == 1 and chunk + 2 < CHUNKS else None
                    if ahead:
                        transpose(ahead)
                        gather(ahead, 0, "scalar" if chunk == 2 else "vector")
                    project(chunk, unit, h0, h1)
                    add_bias(chunk, unit, h0, h1)
                    if h0 == 0 and unit == 0 and chunk + 1 < CHUNKS:
                        quantise(("w", chunk + 1))
                    if ahead:
                        gather(ahead, 1, "scalar")
                if (place, unit) == (1, 0):
                    scalar_norms(0, X_UNITS - 1, range(CHUNK_HEADS))
                if place > 0:
                    close(place, unit)
                if unit in pool_units(place):
                    pool_square(chunk, unit, h0, h1, fold=place < whole)
                elif place == 0:
                    if unit > 0:
                        scalar_norms(chunk, unit - 1, range(h0, h1))
                elif place in by_heads and unit in late_units:
                    if unit == X_UNITS - 1:
                        for late in late_units:
                            scalar_norms(chunk, late, range(h0, h0 + half))
                elif place < final or unit < X_UNITS - 1:
                    scalar_norms(chunk, unit, range(h0, h1))

        vector_squares(chunk, X_UNITS - 1, h0, h1)
        for unit in pool_units(final):
            vector_sums(chunk, unit, h0, h1)
        vector_sums(chunk, X_UNITS - 1, h0, h1)
        finish(chunk, h0, h1, pieces=half)
